import numpy as np
import ml_dtypes


def mxq(x, axis, fmt="e4m3"):
    dtype, down = {"e4m3": (ml_dtypes.float8_e4m3fn, 7), "e5m2": (ml_dtypes.float8_e5m2, 14)}[fmt]
    v = np.moveaxis(np.asarray(x, np.float32).astype(ml_dtypes.bfloat16).astype(np.float64), axis, -1)
    blocks = v.reshape(v.shape[:-1] + (-1, 32))
    amax = np.abs(blocks).max(-1, keepdims=True)
    byte = np.maximum(np.where(amax > 0, np.frexp(amax)[1] - 1 + 127, 0) - down, 1)
    scale = np.exp2(byte - 127.0)
    codes = (blocks / scale).astype(np.float32).astype(dtype).astype(np.float64)
    return np.moveaxis((codes * scale).reshape(v.shape), -1, axis)


WIDE = False


def mx_kscale(k):
    if not WIDE:
        return np.ones(k)
    levels = np.array([10, -10, 5, -5, 0])
    a = np.random.permutation(np.resize(levels, k // 512 * 4)).reshape(k // 512, 4)
    idx = np.arange(k)
    return np.exp2(a[idx // 512, idx % 128 // 32])


BF16 = ml_dtypes.bfloat16


def bf(x):
    return np.asarray(x, np.float32).astype(BF16)


def f64(x):
    return np.asarray(x).astype(np.float64)


R, D = 4096, 1024
NUM_CLASSES = 85


def setup_inputs():
    s = mx_kscale(D)
    k = NUM_CLASSES + 1
    return {
        "x": bf(np.random.standard_normal((R, D)) * s),
        "W_cls": bf(np.random.standard_normal((D, k)) * 0.03 / s[:, None]),
        "b_cls": bf(np.random.standard_normal(k) * 0.1),
        "W_bbox": bf(np.random.standard_normal((D, NUM_CLASSES * 4)) * 0.01 / s[:, None]),
        "b_bbox": bf(np.random.standard_normal(NUM_CLASSES * 4) * 0.1),
        "W_iou": bf(np.random.standard_normal((D, k)) * 0.03 / s[:, None]),
        "b_iou": bf(np.random.standard_normal(k) * 0.1),
    }


def reference(x, W_cls, b_cls, W_bbox, b_bbox, W_iou, b_iou):
    W = np.concatenate([f64(W_cls), f64(W_bbox), f64(W_iou)], axis=1)
    b = np.concatenate([f64(b_cls), f64(b_bbox), f64(b_iou)], axis=0)
    out = (mxq(f64(x), 1, "e4m3") @ mxq(W, 0, "e4m3")) + b
    k = NUM_CLASSES + 1
    scores = out[:, :k]
    deltas = out[:, k:k + NUM_CLASSES * 4]
    ious = out[:, k + NUM_CLASSES * 4:]
    return scores, deltas, ious

@@ -1,0 +1,213 @@
+from contextlib import ExitStack
+
+import concourse.mybir as mybir
+from concourse.masks import make_identity
+
+F32 = mybir.dt.float32
+BF16 = mybir.dt.bfloat16
+U32 = mybir.dt.uint32
+U8 = mybir.dt.uint8
+FP8X4 = mybir.dt.float8_e4m3fn_x4
+ADD = mybir.AluOpType.add
+
+P = 128
+R = 4096
+D = 1024
+NC = 86
+NB = 340
+N = 512
+TILES = R // P
+G = 4
+GROUPS = TILES // G
+FLOPS = 2 * R * D * N
+
+PIN = False
+LOAD_CHUNKS = [1, 1, 2, 4, 8, 8, 8]
+STORE_CHUNKS = [16, 8, 4, 4]
+
+
+def tile_fastrcnnoutputlayersiou_kernel(
+    tc, x, W_cls, b_cls, W_bbox, b_bbox, W_iou, b_iou, out_0, out_1, out_2
+):
+    nc = tc.nc
+    with ExitStack() as ctx:
+        if PIN:
+            ctx.enter_context(tc.manual_schedule())
+        const = ctx.enter_context(tc.tile_pool(name="const", bufs=1))
+        stage = ctx.enter_context(tc.tile_pool(name="stage", bufs=3))
+        xt_pool = ctx.enter_context(tc.psum_pool(name="xtp", bufs=4))
+        acc_pool = ctx.enter_context(tc.psum_pool(name="accp", bufs=4))
+
+        brow = const.tile([P, 768], BF16, name="brow")
+        nc.vector.memset(brow[:], 0.0)
+        ones = const.tile([P, P], BF16, name="ones")
+        nc.vector.memset(ones[:], 1.0)
+        ident = const.tile([P, P], F32, name="ident")
+        make_identity(nc, ident[:])
+
+        nc.scalar.dma_start(out=brow[0:1, 0:NC], in_=b_cls.unsqueeze(0))
+        nc.scalar.dma_start(out=brow[0:1, 96 : 96 + NC], in_=b_iou.unsqueeze(0))
+        nc.scalar.dma_start(out=brow[0:1, 256 : 256 + NB], in_=b_bbox.unsqueeze(0))
+
+        raws = []
+        for nm, w, cw in (("cls", W_cls, NC), ("iou", W_iou, NC), ("bbox", W_bbox, NB)):
+            raw = const.tile([P, 8 * cw], BF16, name="raw_" + nm)
+            nc.sync.dma_start(
+                out=raw[:].rearrange("p (a r) -> p a r", a=4),
+                in_=w.rearrange("(a q e) c -> q a (e c)", a=4, e=2),
+            )
+            raws.append(raw)
+
+        x_view = x.rearrange("(p j) k -> p j k", j=TILES)
+        x_of = []
+        t0 = 0
+        for ci, n in enumerate(LOAD_CHUNKS):
+            xc = const.tile([P, n * D], BF16, name="x%d" % ci)
+            nc.sync.dma_start(
+                out=xc[:], in_=x_view[:, t0 : t0 + n, :].rearrange("p j k -> p (j k)")
+            )
+            for i in range(n):
+                x_of.append((xc, i * (D // 2)))
+            t0 += n
+
+        wg = const.tile([P, 2 * N * 4], BF16, name="wg", align_bytes=64)
+        w_codes = const.tile([P, 2 * N], U32, name="w_codes", align_bytes=64)
+        w_scales = const.tile([P, 2 * N], U8, name="w_scales", align_bytes=64)
+        wg_v = wg[:].rearrange("p (g n t) -> p g n t", g=2, t=4)
+        for g in range(2):
+            for wi, n0 in ((0, 0), (1, NC)):
+                nc.scalar.copy(
+                    out=wg_v[:, g, n0 : n0 + NC, :],
+                    in_=raws[wi][:].rearrange("p (g t c) -> p g c t", g=2, t=4)[:, g],
+                )
+            nc.vector.tensor_copy(
+                out=wg_v[:, g, 2 * NC : N, :].rearrange("p (c i) t -> p c t i", i=4),
+                in_=raws[2][:].rearrange("p (g t c i) -> p g c t i", g=2, t=4, i=4)[:, g],
+            )
+        for g in range(2):
+            nc.vector.quantize_mx(
+                out=w_codes[:, g * N : (g + 1) * N].bitcast(FP8X4),
+                scales=w_scales[:, g * N : (g + 1) * N],
+                in_=wg[:, g * 4 * N : (g + 1) * 4 * N],
+            )
+
+        bias = const.tile([P, 768], F32, name="bias")
+
+        def bias_spread():
+            pa = acc_pool.tile([P, N], F32, name="pa", tag="acc")
+            nc.tensor.matmul(pa[:, 0:256], lhsT=ones[:], rhs=brow[:, 0:256], start=True, stop=True)
+            pb = acc_pool.tile([P, N], F32, name="pb", tag="acc")
+            nc.tensor.matmul(pb[:], lhsT=ones[:], rhs=brow[:, 256:768], start=True, stop=True)
+            nc.scalar.copy(out=bias[:, 0:256], in_=pa[:, 0:256])
+            nc.scalar.copy(out=bias[:, 256:768], in_=pb[:])
+
+        bias_small = bias[:, 0:192].rearrange("p (h c) -> p h c", h=2)[:, :, 0:NC]
+        bias_bbox = bias[:, 256 : 256 + NB]
+
+        res_of = []
+        store_at = {}
+        t0 = 0
+        for si, n in enumerate(STORE_CHUNKS):
+            s02 = const.tile([P, 2 * n * NC], F32, name="s02_%d" % si)
+            s1 = const.tile([P, n * NB], F32, name="s1_%d" % si)
+            for j in range(n):
+                res_of.append(
+                    (
+                        s02[:].rearrange("p (h j c) -> p h j c", h=2, j=n)[:, :, j, :],
+                        s1[:, j * NB : (j + 1) * NB],
+                    )
+                )
+            store_at[t0 + n - 1] = (t0, n, s02, s1)
+            t0 += n
+
+        o0 = out_0.rearrange("(p j) c -> p (j c)", j=TILES)
+        o1 = out_1.rearrange("(p j) c -> p (j c)", j=TILES)
+        o2 = out_2.rearrange("(p j) c -> p (j c)", j=TILES)
+
+        grouped = {}
+        codes = {}
+        planes = {}
+        banks = {}
+        accs = {}
+
+        def transposes(c):
+            for i in range(G):
+                xc, w0 = x_of[c * G + i]
+                xt = xt_pool.tile([P, 4, P], F32, name="xt", tag="xt")
+                for a in range(4):
+                    nc.tensor.transpose(
+                        xt[:, a, :],
+                        xc[:].bitcast(F32)[:, w0 + a * P : w0 + (a + 1) * P],
+                        ident[:],
+                    )
+                banks[c * G + i] = xt
+
+        def exits(c):
+            xg = stage.tile([P, G * D], BF16, name="xg", tag="xg", align_bytes=64)
+            grouped[c] = xg
+            for i in range(G):
+                nc.scalar.copy(
+                    out=xg[:]
+                    .bitcast(F32)[:, i * (D // 2) : (i + 1) * (D // 2)]
+                    .rearrange("p (g m u) -> p g m u", g=2, u=2),
+                    in_=banks[c * G + i][:].rearrange("p (g u) m -> p g m u", u=2),
+                )
+            codes[c] = stage.tile([P, G * 256], U32, name="xq", tag="xq", align_bytes=64)
+            planes[c] = stage.tile([P, G * 256], U8, name="xs", tag="xs", align_bytes=64)
+
+        def quantise(c, h):
+            nc.vector.quantize_mx(
+                out=codes[c][:, h * 512 : (h + 1) * 512].bitcast(FP8X4),
+                scales=planes[c][:, h * 512 : (h + 1) * 512],
+                in_=grouped[c][:, h * 2048 : (h + 1) * 2048],
+            )
+
+        def passes(c):
+            for i in range(G):
+                acc = acc_pool.tile([P, N], F32, name="acc", tag="acc")
+                accs[c * G + i] = acc
+                for g in range(2):
+                    lo = i * 256 + g * P
+                    nc.tensor.matmul_mx(
+                        out=acc[:],
+                        lhsT=codes[c][:, lo : lo + P].bitcast(FP8X4),
+                        lhsT_scale=planes[c][:, lo : lo + P],
+                        rhs=w_codes[:, g * N : (g + 1) * N].bitcast(FP8X4),
+                        rhs_scale=w_scales[:, g * N : (g + 1) * N],
+                        start=(g == 0),
+                        stop=(g == 1),
+                    )
+
+        def finish(t):
+            small, bbox = res_of[t]
+            acc = accs[t]
+            nc.vector.tensor_tensor(
+                out=bbox, in0=acc[:, 2 * NC : N], in1=bias_bbox, op=ADD
+            )
+            nc.vector.tensor_tensor(
+                out=small,
+                in0=acc[:, 0 : 2 * NC].rearrange("p (h c) -> p h c", h=2),
+                in1=bias_small,
+                op=ADD,
+            )
+            if t in store_at:
+                s0, n, s02, s1 = store_at[t]
+                nc.sync.dma_start(out=o1[:, s0 * NB : (s0 + n) * NB], in_=s1[:])
+                nc.sync.dma_start(out=o0[:, s0 * NC : (s0 + n) * NC], in_=s02[:, 0 : n * NC])
+                nc.sync.dma_start(out=o2[:, s0 * NC : (s0 + n) * NC], in_=s02[:, n * NC : 2 * n * NC])
+
+        transposes(0)
+        exits(0)
+        bias_spread()
+        quantise(0, 0)
+        quantise(0, 1)
+        for c in range(GROUPS):
+            if c + 1 < GROUPS:
+                transposes(c + 1)
+                exits(c + 1)
+            passes(c)
+            for h in range(2):
+                finish(c * G + 2 * h)
+                finish(c * G + 2 * h + 1)
+                if c + 1 < GROUPS:
+                    quantise(c + 1, h)

@@ -17,13 +17,13 @@ NC = 86
 NB = 340
 N = 512
 TILES = R // P
-G = 4
-GROUPS = TILES // G
 FLOPS = 2 * R * D * N
 
-PIN = False
+PIN = True
 LOAD_CHUNKS = [1, 1, 2, 4, 8, 8, 8]
-STORE_CHUNKS = [16, 8, 4, 4]
+STORE_CHUNKS = [("bbox", [8, 8, 4, 4, 4, 4]), ("small", [8, 8, 4, 4, 4, 4])]
+RUNS = [2] * 8
+STAGE_BUFS = 6
 
 
 def tile_fastrcnnoutputlayersiou_kernel(
@@ -34,7 +34,7 @@ def tile_fastrcnnoutputlayersiou_kernel(
         if PIN:
             ctx.enter_context(tc.manual_schedule())
         const = ctx.enter_context(tc.tile_pool(name="const", bufs=1))
-        stage = ctx.enter_context(tc.tile_pool(name="stage", bufs=3))
+        stage = ctx.enter_context(tc.tile_pool(name="stage", bufs=STAGE_BUFS))
         xt_pool = ctx.enter_context(tc.psum_pool(name="xtp", bufs=4))
         acc_pool = ctx.enter_context(tc.psum_pool(name="accp", bufs=4))
 
@@ -49,14 +49,14 @@ def tile_fastrcnnoutputlayersiou_kernel(
         nc.scalar.dma_start(out=brow[0:1, 96 : 96 + NC], in_=b_iou.unsqueeze(0))
         nc.scalar.dma_start(out=brow[0:1, 256 : 256 + NB], in_=b_bbox.unsqueeze(0))
 
-        raws = []
-        for nm, w, cw in (("cls", W_cls, NC), ("iou", W_iou, NC), ("bbox", W_bbox, NB)):
+        raws = {}
+        for nm, w, cw in (("bbox", W_bbox, NB), ("cls", W_cls, NC), ("iou", W_iou, NC)):
             raw = const.tile([P, 8 * cw], BF16, name="raw_" + nm)
             nc.sync.dma_start(
                 out=raw[:].rearrange("p (a r) -> p a r", a=4),
                 in_=w.rearrange("(a q e) c -> q a (e c)", a=4, e=2),
             )
-            raws.append(raw)
+            raws[nm] = raw
 
         x_view = x.rearrange("(p j) k -> p j k", j=TILES)
         x_of = []
@@ -75,15 +75,16 @@ def tile_fastrcnnoutputlayersiou_kernel(
         w_scales = const.tile([P, 2 * N], U8, name="w_scales", align_bytes=64)
         wg_v = wg[:].rearrange("p (g n t) -> p g n t", g=2, t=4)
         for g in range(2):
-            for wi, n0 in ((0, 0), (1, NC)):
-                nc.scalar.copy(
-                    out=wg_v[:, g, n0 : n0 + NC, :],
-                    in_=raws[wi][:].rearrange("p (g t c) -> p g c t", g=2, t=4)[:, g],
-                )
             nc.vector.tensor_copy(
                 out=wg_v[:, g, 2 * NC : N, :].rearrange("p (c i) t -> p c t i", i=4),
-                in_=raws[2][:].rearrange("p (g t c i) -> p g c t i", g=2, t=4, i=4)[:, g],
+                in_=raws["bbox"][:].rearrange("p (g t c i) -> p g c t i", g=2, t=4, i=4)[:, g],
             )
+        for nm, n0 in (("cls", 0), ("iou", NC)):
+            for g in range(2):
+                nc.scalar.copy(
+                    out=wg_v[:, g, n0 : n0 + NC, :],
+                    in_=raws[nm][:].rearrange("p (g t c) -> p g c t", g=2, t=4)[:, g],
+                )
         for g in range(2):
             nc.vector.quantize_mx(
                 out=w_codes[:, g * N : (g + 1) * N].bitcast(FP8X4),
@@ -104,25 +105,31 @@ def tile_fastrcnnoutputlayersiou_kernel(
         bias_small = bias[:, 0:192].rearrange("p (h c) -> p h c", h=2)[:, :, 0:NC]
         bias_bbox = bias[:, 256 : 256 + NB]
 
-        res_of = []
+        res_small = []
+        res_bbox = []
         store_at = {}
-        t0 = 0
-        for si, n in enumerate(STORE_CHUNKS):
-            s02 = const.tile([P, 2 * n * NC], F32, name="s02_%d" % si)
-            s1 = const.tile([P, n * NB], F32, name="s1_%d" % si)
-            for j in range(n):
-                res_of.append(
-                    (
-                        s02[:].rearrange("p (h j c) -> p h j c", h=2, j=n)[:, :, j, :],
-                        s1[:, j * NB : (j + 1) * NB],
-                    )
-                )
-            store_at[t0 + n - 1] = (t0, n, s02, s1)
-            t0 += n
-
         o0 = out_0.rearrange("(p j) c -> p (j c)", j=TILES)
         o1 = out_1.rearrange("(p j) c -> p (j c)", j=TILES)
         o2 = out_2.rearrange("(p j) c -> p (j c)", j=TILES)
+        for kind, chunks in STORE_CHUNKS:
+            t0 = 0
+            for si, n in enumerate(chunks):
+                todo = store_at.get(t0 + n - 1, [])
+                if kind == "small":
+                    s02 = const.tile([P, 2 * n * NC], F32, name="s02_%d" % si)
+                    for j in range(n):
+                        res_small.append(
+                            s02[:].rearrange("p (h j c) -> p h j c", h=2, j=n)[:, :, j, :]
+                        )
+                    todo.append((o0[:, t0 * NC : (t0 + n) * NC], s02[:, 0 : n * NC]))
+                    todo.append((o2[:, t0 * NC : (t0 + n) * NC], s02[:, n * NC : 2 * n * NC]))
+                else:
+                    s1 = const.tile([P, n * NB], F32, name="s1_%d" % si)
+                    for j in range(n):
+                        res_bbox.append(s1[:, j * NB : (j + 1) * NB])
+                    todo.append((o1[:, t0 * NB : (t0 + n) * NB], s1[:]))
+                store_at[t0 + n - 1] = todo
+                t0 += n
 
         grouped = {}
         codes = {}
@@ -130,9 +137,9 @@ def tile_fastrcnnoutputlayersiou_kernel(
         banks = {}
         accs = {}
 
-        def transposes(c):
-            for i in range(G):
-                xc, w0 = x_of[c * G + i]
+        def transposes(q):
+            for t in (2 * q, 2 * q + 1):
+                xc, w0 = x_of[t]
                 xt = xt_pool.tile([P, 4, P], F32, name="xt", tag="xt")
                 for a in range(4):
                     nc.tensor.transpose(
@@ -140,74 +147,81 @@ def tile_fastrcnnoutputlayersiou_kernel(
                         xc[:].bitcast(F32)[:, w0 + a * P : w0 + (a + 1) * P],
                         ident[:],
                     )
-                banks[c * G + i] = xt
+                banks[t] = xt
 
-        def exits(c):
-            xg = stage.tile([P, G * D], BF16, name="xg", tag="xg", align_bytes=64)
-            grouped[c] = xg
-            for i in range(G):
+        def exits(q):
+            xg = stage.tile([P, 2 * D], BF16, name="xg", tag="xg", align_bytes=64)
+            grouped[q] = xg
+            for i in range(2):
                 nc.scalar.copy(
                     out=xg[:]
                     .bitcast(F32)[:, i * (D // 2) : (i + 1) * (D // 2)]
                     .rearrange("p (g m u) -> p g m u", g=2, u=2),
-                    in_=banks[c * G + i][:].rearrange("p (g u) m -> p g m u", u=2),
+                    in_=banks[2 * q + i][:].rearrange("p (g u) m -> p g m u", u=2),
                 )
-            codes[c] = stage.tile([P, G * 256], U32, name="xq", tag="xq", align_bytes=64)
-            planes[c] = stage.tile([P, G * 256], U8, name="xs", tag="xs", align_bytes=64)
 
-        def quantise(c, h):
+        def quantise(q):
+            codes[q] = stage.tile([P, 512], U32, name="xq", tag="xq", align_bytes=64)
+            planes[q] = stage.tile([P, 512], U8, name="xs", tag="xs", align_bytes=64)
             nc.vector.quantize_mx(
-                out=codes[c][:, h * 512 : (h + 1) * 512].bitcast(FP8X4),
-                scales=planes[c][:, h * 512 : (h + 1) * 512],
-                in_=grouped[c][:, h * 2048 : (h + 1) * 2048],
+                out=codes[q][:].bitcast(FP8X4), scales=planes[q][:], in_=grouped[q][:]
             )
 
-        def passes(c):
-            for i in range(G):
+        def passes(q):
+            for i in range(2):
                 acc = acc_pool.tile([P, N], F32, name="acc", tag="acc")
-                accs[c * G + i] = acc
+                accs[2 * q + i] = acc
                 for g in range(2):
                     lo = i * 256 + g * P
                     nc.tensor.matmul_mx(
                         out=acc[:],
-                        lhsT=codes[c][:, lo : lo + P].bitcast(FP8X4),
-                        lhsT_scale=planes[c][:, lo : lo + P],
+                        lhsT=codes[q][:, lo : lo + P].bitcast(FP8X4),
+                        lhsT_scale=planes[q][:, lo : lo + P],
                         rhs=w_codes[:, g * N : (g + 1) * N].bitcast(FP8X4),
                         rhs_scale=w_scales[:, g * N : (g + 1) * N],
                         start=(g == 0),
                         stop=(g == 1),
                     )
 
-        def finish(t):
-            small, bbox = res_of[t]
-            acc = accs[t]
-            nc.vector.tensor_tensor(
-                out=bbox, in0=acc[:, 2 * NC : N], in1=bias_bbox, op=ADD
-            )
-            nc.vector.tensor_tensor(
-                out=small,
-                in0=acc[:, 0 : 2 * NC].rearrange("p (h c) -> p h c", h=2),
-                in1=bias_small,
-                op=ADD,
-            )
-            if t in store_at:
-                s0, n, s02, s1 = store_at[t]
-                nc.sync.dma_start(out=o1[:, s0 * NB : (s0 + n) * NB], in_=s1[:])
-                nc.sync.dma_start(out=o0[:, s0 * NC : (s0 + n) * NC], in_=s02[:, 0 : n * NC])
-                nc.sync.dma_start(out=o2[:, s0 * NC : (s0 + n) * NC], in_=s02[:, n * NC : 2 * n * NC])
+        def finish(q):
+            for t in (2 * q, 2 * q + 1):
+                acc = accs[t]
+                nc.vector.tensor_tensor(
+                    out=res_bbox[t], in0=acc[:, 2 * NC : N], in1=bias_bbox, op=ADD
+                )
+                nc.vector.tensor_tensor(
+                    out=res_small[t],
+                    in0=acc[:, 0 : 2 * NC].rearrange("p (h c) -> p h c", h=2),
+                    in1=bias_small,
+                    op=ADD,
+                )
+                for dst, src in store_at.get(t, []):
+                    nc.sync.dma_start(out=dst, in_=src)
 
-        transposes(0)
-        exits(0)
+        runs = []
+        q0 = 0
+        for n in RUNS:
+            runs.append(list(range(q0, q0 + n)))
+            q0 += n
+        assert q0 * 2 == TILES
+
+        for q in runs[0]:
+            transposes(q)
+        for q in runs[0]:
+            exits(q)
         bias_spread()
-        quantise(0, 0)
-        quantise(0, 1)
-        for c in range(GROUPS):
-            if c + 1 < GROUPS:
-                transposes(c + 1)
-                exits(c + 1)
-            passes(c)
-            for h in range(2):
-                finish(c * G + 2 * h)
-                finish(c * G + 2 * h + 1)
-                if c + 1 < GROUPS:
-                    quantise(c + 1, h)
+        for q in runs[0]:
+            quantise(q)
+        for k, cur in enumerate(runs):
+            nxt = runs[k + 1] if k + 1 < len(runs) else []
+            for q in nxt:
+                transposes(q)
+            for q in nxt:
+                exits(q)
+            for q in cur:
+                passes(q)
+            for i in range(max(len(cur), len(nxt))):
+                if i < len(nxt):
+                    quantise(nxt[i])
+                if i < len(cur):
+                    finish(cur[i])

@@ -20,9 +20,10 @@ TILES = R // P
 FLOPS = 2 * R * D * N
 
 PIN = True
-LOAD_CHUNKS = [1, 1, 2, 4, 8, 8, 8]
+LOAD_CHUNKS = [1, 1, 1, 1, 2, 2, 4, 4, 8, 8]
 STORE_CHUNKS = [("bbox", [8, 8, 4, 4, 4, 4]), ("small", [8, 8, 4, 4, 4, 4])]
-RUNS = [2] * 8
+RUNS = [1, 1, 1, 1] + [2] * 6
+SPLIT_Q = (0,)
 STAGE_BUFS = 6
 
 
@@ -94,11 +95,12 @@ def tile_fastrcnnoutputlayersiou_kernel(
 
         bias = const.tile([P, 768], F32, name="bias")
 
+        pa = acc_pool.tile([P, N], F32, name="pa", tag="acc")
+        nc.tensor.matmul(pa[:, 0:256], lhsT=ones[:], rhs=brow[:, 0:256], start=True, stop=True)
+        pb = acc_pool.tile([P, N], F32, name="pb", tag="acc")
+        nc.tensor.matmul(pb[:], lhsT=ones[:], rhs=brow[:, 256:768], start=True, stop=True)
+
         def bias_spread():
-            pa = acc_pool.tile([P, N], F32, name="pa", tag="acc")
-            nc.tensor.matmul(pa[:, 0:256], lhsT=ones[:], rhs=brow[:, 0:256], start=True, stop=True)
-            pb = acc_pool.tile([P, N], F32, name="pb", tag="acc")
-            nc.tensor.matmul(pb[:], lhsT=ones[:], rhs=brow[:, 256:768], start=True, stop=True)
             nc.scalar.copy(out=bias[:, 0:256], in_=pa[:, 0:256])
             nc.scalar.copy(out=bias[:, 256:768], in_=pb[:])
 
@@ -163,9 +165,14 @@ def tile_fastrcnnoutputlayersiou_kernel(
         def quantise(q):
             codes[q] = stage.tile([P, 512], U32, name="xq", tag="xq", align_bytes=64)
             planes[q] = stage.tile([P, 512], U8, name="xs", tag="xs", align_bytes=64)
-            nc.vector.quantize_mx(
-                out=codes[q][:].bitcast(FP8X4), scales=planes[q][:], in_=grouped[q][:]
-            )
+            cuts = 2 if q in SPLIT_Q else 1
+            w = 512 // cuts
+            for s in range(cuts):
+                nc.vector.quantize_mx(
+                    out=codes[q][:, s * w : (s + 1) * w].bitcast(FP8X4),
+                    scales=planes[q][:, s * w : (s + 1) * w],
+                    in_=grouped[q][:, s * 4 * w : (s + 1) * 4 * w],
+                )
 
         def passes(q):
             for i in range(2):
@@ -209,7 +216,6 @@ def tile_fastrcnnoutputlayersiou_kernel(
             transposes(q)
         for q in runs[0]:
             exits(q)
-        bias_spread()
         for q in runs[0]:
             quantise(q)
         for k, cur in enumerate(runs):
@@ -218,6 +224,8 @@ def tile_fastrcnnoutputlayersiou_kernel(
                 transposes(q)
             for q in nxt:
                 exits(q)
+            if k == 0:
+                bias_spread()
             for q in cur:
                 passes(q)
             for i in range(max(len(cur), len(nxt))):

@@ -21,7 +21,7 @@ FLOPS = 2 * R * D * N
 
 PIN = True
 LOAD_CHUNKS = [1, 1, 1, 1, 2, 2, 4, 4, 8, 8]
-STORE_CHUNKS = [("bbox", [8, 8, 4, 4, 4, 4]), ("small", [8, 8, 4, 4, 4, 4])]
+STORE_CHUNKS = [("bbox", [8, 8, 4, 4, 4, 2, 2]), ("small", [16, 8, 4, 4])]
 RUNS = [1, 1, 1, 1] + [2] * 6
 SPLIT_Q = (0,)
 STAGE_BUFS = 6
@@ -39,7 +39,7 @@ def tile_fastrcnnoutputlayersiou_kernel(
         xt_pool = ctx.enter_context(tc.psum_pool(name="xtp", bufs=4))
         acc_pool = ctx.enter_context(tc.psum_pool(name="accp", bufs=4))
 
-        brow = const.tile([P, 768], BF16, name="brow")
+        brow = const.tile([P, N], BF16, name="brow")
         nc.vector.memset(brow[:], 0.0)
         ones = const.tile([P, P], BF16, name="ones")
         nc.vector.memset(ones[:], 1.0)
@@ -47,8 +47,8 @@ def tile_fastrcnnoutputlayersiou_kernel(
         make_identity(nc, ident[:])
 
         nc.scalar.dma_start(out=brow[0:1, 0:NC], in_=b_cls.unsqueeze(0))
-        nc.scalar.dma_start(out=brow[0:1, 96 : 96 + NC], in_=b_iou.unsqueeze(0))
-        nc.scalar.dma_start(out=brow[0:1, 256 : 256 + NB], in_=b_bbox.unsqueeze(0))
+        nc.scalar.dma_start(out=brow[1:2, NC : 2 * NC], in_=b_iou.unsqueeze(0))
+        nc.scalar.dma_start(out=brow[2:3, 2 * NC : N], in_=b_bbox.unsqueeze(0))
 
         raws = {}
         for nm, w, cw in (("bbox", W_bbox, NB), ("cls", W_cls, NC), ("iou", W_iou, NC)):
@@ -93,44 +93,41 @@ def tile_fastrcnnoutputlayersiou_kernel(
                 in_=wg[:, g * 4 * N : (g + 1) * 4 * N],
             )
 
-        bias = const.tile([P, 768], F32, name="bias")
-
-        pa = acc_pool.tile([P, N], F32, name="pa", tag="acc")
-        nc.tensor.matmul(pa[:, 0:256], lhsT=ones[:], rhs=brow[:, 0:256], start=True, stop=True)
-        pb = acc_pool.tile([P, N], F32, name="pb", tag="acc")
-        nc.tensor.matmul(pb[:], lhsT=ones[:], rhs=brow[:, 256:768], start=True, stop=True)
+        bias = const.tile([P, N], F32, name="bias")
 
         def bias_spread():
-            nc.scalar.copy(out=bias[:, 0:256], in_=pa[:, 0:256])
-            nc.scalar.copy(out=bias[:, 256:768], in_=pb[:])
+            pb = acc_pool.tile([P, N], F32, name="pb", tag="acc")
+            nc.tensor.matmul(pb[:], lhsT=ones[:], rhs=brow[:], start=True, stop=True)
+            nc.scalar.copy(out=bias[:], in_=pb[:])
 
-        bias_small = bias[:, 0:192].rearrange("p (h c) -> p h c", h=2)[:, :, 0:NC]
-        bias_bbox = bias[:, 256 : 256 + NB]
+        bias_small = bias[:, 0 : 2 * NC].rearrange("p (h c) -> p h c", h=2)
+        bias_bbox = bias[:, 2 * NC : N]
 
         res_small = []
         res_bbox = []
-        store_at = {}
+        store_bbox = {}
+        store_small = {}
         o0 = out_0.rearrange("(p j) c -> p (j c)", j=TILES)
         o1 = out_1.rearrange("(p j) c -> p (j c)", j=TILES)
         o2 = out_2.rearrange("(p j) c -> p (j c)", j=TILES)
         for kind, chunks in STORE_CHUNKS:
             t0 = 0
             for si, n in enumerate(chunks):
-                todo = store_at.get(t0 + n - 1, [])
                 if kind == "small":
                     s02 = const.tile([P, 2 * n * NC], F32, name="s02_%d" % si)
                     for j in range(n):
                         res_small.append(
                             s02[:].rearrange("p (h j c) -> p h j c", h=2, j=n)[:, :, j, :]
                         )
-                    todo.append((o0[:, t0 * NC : (t0 + n) * NC], s02[:, 0 : n * NC]))
-                    todo.append((o2[:, t0 * NC : (t0 + n) * NC], s02[:, n * NC : 2 * n * NC]))
+                    store_small[t0 + n - 1] = [
+                        (o0[:, t0 * NC : (t0 + n) * NC], s02[:, 0 : n * NC]),
+                        (o2[:, t0 * NC : (t0 + n) * NC], s02[:, n * NC : 2 * n * NC]),
+                    ]
                 else:
                     s1 = const.tile([P, n * NB], F32, name="s1_%d" % si)
                     for j in range(n):
                         res_bbox.append(s1[:, j * NB : (j + 1) * NB])
-                    todo.append((o1[:, t0 * NB : (t0 + n) * NB], s1[:]))
-                store_at[t0 + n - 1] = todo
+                    store_bbox[t0 + n - 1] = [(o1[:, t0 * NB : (t0 + n) * NB], s1[:])]
                 t0 += n
 
         grouped = {}
@@ -196,13 +193,15 @@ def tile_fastrcnnoutputlayersiou_kernel(
                 nc.vector.tensor_tensor(
                     out=res_bbox[t], in0=acc[:, 2 * NC : N], in1=bias_bbox, op=ADD
                 )
+                for dst, src in store_bbox.get(t, []):
+                    nc.sync.dma_start(out=dst, in_=src)
                 nc.vector.tensor_tensor(
                     out=res_small[t],
                     in0=acc[:, 0 : 2 * NC].rearrange("p (h c) -> p h c", h=2),
                     in1=bias_small,
                     op=ADD,
                 )
-                for dst, src in store_at.get(t, []):
+                for dst, src in store_small.get(t, []):
                     nc.sync.dma_start(out=dst, in_=src)
 
         runs = []

@@ -39,16 +39,15 @@ def tile_fastrcnnoutputlayersiou_kernel(
         xt_pool = ctx.enter_context(tc.psum_pool(name="xtp", bufs=4))
         acc_pool = ctx.enter_context(tc.psum_pool(name="accp", bufs=4))
 
-        brow = const.tile([P, N], BF16, name="brow")
-        nc.vector.memset(brow[:], 0.0)
         ones = const.tile([P, P], BF16, name="ones")
         nc.vector.memset(ones[:], 1.0)
         ident = const.tile([P, P], F32, name="ident")
         make_identity(nc, ident[:])
-
-        nc.scalar.dma_start(out=brow[0:1, 0:NC], in_=b_cls.unsqueeze(0))
-        nc.scalar.dma_start(out=brow[1:2, NC : 2 * NC], in_=b_iou.unsqueeze(0))
-        nc.scalar.dma_start(out=brow[2:3, 2 * NC : N], in_=b_bbox.unsqueeze(0))
+        brow = const.tile([P, N], BF16, name="brow")
+        nc.gpsimd.memset(brow[:].bitcast(F32), 0.0)
+        nc.gpsimd.dma_start(out=brow[0:1, 0:NC], in_=b_cls.unsqueeze(0))
+        nc.gpsimd.dma_start(out=brow[1:2, NC : 2 * NC], in_=b_iou.unsqueeze(0))
+        nc.gpsimd.dma_start(out=brow[2:3, 2 * NC : N], in_=b_bbox.unsqueeze(0))
 
         raws = {}
         for nm, w, cw in (("bbox", W_bbox, NB), ("cls", W_cls, NC), ("iou", W_iou, NC)):

from contextlib import ExitStack

import concourse.mybir as mybir
from concourse.masks import make_identity

F32 = mybir.dt.float32
BF16 = mybir.dt.bfloat16
U32 = mybir.dt.uint32
U8 = mybir.dt.uint8
FP8X4 = mybir.dt.float8_e4m3fn_x4
ADD = mybir.AluOpType.add

P = 128
R = 4096
D = 1024
NC = 86
NB = 340
N = 512
TILES = R // P
FLOPS = 2 * R * D * N

PIN = True
LOAD_CHUNKS = [1, 1, 1, 1, 2, 2, 4, 4, 8, 8]
STORE_CHUNKS = [("bbox", [8, 8, 4, 4, 4, 2, 2]), ("small", [16, 8, 4, 4])]
RUNS = [1, 1, 1, 1] + [2] * 6
SPLIT_Q = (0,)
STAGE_BUFS = 6


def tile_fastrcnnoutputlayersiou_kernel(
    tc, x, W_cls, b_cls, W_bbox, b_bbox, W_iou, b_iou, out_0, out_1, out_2
):
    nc = tc.nc
    with ExitStack() as ctx:
        if PIN:
            ctx.enter_context(tc.manual_schedule())
        const = ctx.enter_context(tc.tile_pool(name="const", bufs=1))
        stage = ctx.enter_context(tc.tile_pool(name="stage", bufs=STAGE_BUFS))
        xt_pool = ctx.enter_context(tc.psum_pool(name="xtp", bufs=4))
        acc_pool = ctx.enter_context(tc.psum_pool(name="accp", bufs=4))

        ones = const.tile([P, P], BF16, name="ones")
        nc.vector.memset(ones[:], 1.0)
        ident = const.tile([P, P], F32, name="ident")
        make_identity(nc, ident[:])
        brow = const.tile([P, N], BF16, name="brow")
        nc.gpsimd.memset(brow[:].bitcast(F32), 0.0)
        nc.gpsimd.dma_start(out=brow[0:1, 0:NC], in_=b_cls.unsqueeze(0))
        nc.gpsimd.dma_start(out=brow[1:2, NC : 2 * NC], in_=b_iou.unsqueeze(0))
        nc.gpsimd.dma_start(out=brow[2:3, 2 * NC : N], in_=b_bbox.unsqueeze(0))

        raws = {}
        for nm, w, cw in (("bbox", W_bbox, NB), ("cls", W_cls, NC), ("iou", W_iou, NC)):
            raw = const.tile([P, 8 * cw], BF16, name="raw_" + nm)
            nc.sync.dma_start(
                out=raw[:].rearrange("p (a r) -> p a r", a=4),
                in_=w.rearrange("(a q e) c -> q a (e c)", a=4, e=2),
            )
            raws[nm] = raw

        x_view = x.rearrange("(p j) k -> p j k", j=TILES)
        x_of = []
        t0 = 0
        for ci, n in enumerate(LOAD_CHUNKS):
            xc = const.tile([P, n * D], BF16, name="x%d" % ci)
            nc.sync.dma_start(
                out=xc[:], in_=x_view[:, t0 : t0 + n, :].rearrange("p j k -> p (j k)")
            )
            for i in range(n):
                x_of.append((xc, i * (D // 2)))
            t0 += n

        wg = const.tile([P, 2 * N * 4], BF16, name="wg", align_bytes=64)
        w_codes = const.tile([P, 2 * N], U32, name="w_codes", align_bytes=64)
        w_scales = const.tile([P, 2 * N], U8, name="w_scales", align_bytes=64)
        wg_v = wg[:].rearrange("p (g n t) -> p g n t", g=2, t=4)
        for g in range(2):
            nc.vector.tensor_copy(
                out=wg_v[:, g, 2 * NC : N, :].rearrange("p (c i) t -> p c t i", i=4),
                in_=raws["bbox"][:].rearrange("p (g t c i) -> p g c t i", g=2, t=4, i=4)[:, g],
            )
        for nm, n0 in (("cls", 0), ("iou", NC)):
            for g in range(2):
                nc.scalar.copy(
                    out=wg_v[:, g, n0 : n0 + NC, :],
                    in_=raws[nm][:].rearrange("p (g t c) -> p g c t", g=2, t=4)[:, g],
                )
        for g in range(2):
            nc.vector.quantize_mx(
                out=w_codes[:, g * N : (g + 1) * N].bitcast(FP8X4),
                scales=w_scales[:, g * N : (g + 1) * N],
                in_=wg[:, g * 4 * N : (g + 1) * 4 * N],
            )

        bias = const.tile([P, N], F32, name="bias")

        def bias_spread():
            pb = acc_pool.tile([P, N], F32, name="pb", tag="acc")
            nc.tensor.matmul(pb[:], lhsT=ones[:], rhs=brow[:], start=True, stop=True)
            nc.scalar.copy(out=bias[:], in_=pb[:])

        bias_small = bias[:, 0 : 2 * NC].rearrange("p (h c) -> p h c", h=2)
        bias_bbox = bias[:, 2 * NC : N]

        res_small = []
        res_bbox = []
        store_bbox = {}
        store_small = {}
        o0 = out_0.rearrange("(p j) c -> p (j c)", j=TILES)
        o1 = out_1.rearrange("(p j) c -> p (j c)", j=TILES)
        o2 = out_2.rearrange("(p j) c -> p (j c)", j=TILES)
        for kind, chunks in STORE_CHUNKS:
            t0 = 0
            for si, n in enumerate(chunks):
                if kind == "small":
                    s02 = const.tile([P, 2 * n * NC], F32, name="s02_%d" % si)
                    for j in range(n):
                        res_small.append(
                            s02[:].rearrange("p (h j c) -> p h j c", h=2, j=n)[:, :, j, :]
                        )
                    store_small[t0 + n - 1] = [
                        (o0[:, t0 * NC : (t0 + n) * NC], s02[:, 0 : n * NC]),
                        (o2[:, t0 * NC : (t0 + n) * NC], s02[:, n * NC : 2 * n * NC]),
                    ]
                else:
                    s1 = const.tile([P, n * NB], F32, name="s1_%d" % si)
                    for j in range(n):
                        res_bbox.append(s1[:, j * NB : (j + 1) * NB])
                    store_bbox[t0 + n - 1] = [(o1[:, t0 * NB : (t0 + n) * NB], s1[:])]
                t0 += n

        grouped = {}
        codes = {}
        planes = {}
        banks = {}
        accs = {}

        def transposes(q):
            for t in (2 * q, 2 * q + 1):
                xc, w0 = x_of[t]
                xt = xt_pool.tile([P, 4, P], F32, name="xt", tag="xt")
                for a in range(4):
                    nc.tensor.transpose(
                        xt[:, a, :],
                        xc[:].bitcast(F32)[:, w0 + a * P : w0 + (a + 1) * P],
                        ident[:],
                    )
                banks[t] = xt

        def exits(q):
            xg = stage.tile([P, 2 * D], BF16, name="xg", tag="xg", align_bytes=64)
            grouped[q] = xg
            for i in range(2):
                nc.scalar.copy(
                    out=xg[:]
                    .bitcast(F32)[:, i * (D // 2) : (i + 1) * (D // 2)]
                    .rearrange("p (g m u) -> p g m u", g=2, u=2),
                    in_=banks[2 * q + i][:].rearrange("p (g u) m -> p g m u", u=2),
                )

        def quantise(q):
            codes[q] = stage.tile([P, 512], U32, name="xq", tag="xq", align_bytes=64)
            planes[q] = stage.tile([P, 512], U8, name="xs", tag="xs", align_bytes=64)
            cuts = 2 if q in SPLIT_Q else 1
            w = 512 // cuts
            for s in range(cuts):
                nc.vector.quantize_mx(
                    out=codes[q][:, s * w : (s + 1) * w].bitcast(FP8X4),
                    scales=planes[q][:, s * w : (s + 1) * w],
                    in_=grouped[q][:, s * 4 * w : (s + 1) * 4 * w],
                )

        def passes(q):
            for i in range(2):
                acc = acc_pool.tile([P, N], F32, name="acc", tag="acc")
                accs[2 * q + i] = acc
                for g in range(2):
                    lo = i * 256 + g * P
                    nc.tensor.matmul_mx(
                        out=acc[:],
                        lhsT=codes[q][:, lo : lo + P].bitcast(FP8X4),
                        lhsT_scale=planes[q][:, lo : lo + P],
                        rhs=w_codes[:, g * N : (g + 1) * N].bitcast(FP8X4),
                        rhs_scale=w_scales[:, g * N : (g + 1) * N],
                        start=(g == 0),
                        stop=(g == 1),
                    )

        def finish(q):
            for t in (2 * q, 2 * q + 1):
                acc = accs[t]
                nc.vector.tensor_tensor(
                    out=res_bbox[t], in0=acc[:, 2 * NC : N], in1=bias_bbox, op=ADD
                )
                for dst, src in store_bbox.get(t, []):
                    nc.sync.dma_start(out=dst, in_=src)
                nc.vector.tensor_tensor(
                    out=res_small[t],
                    in0=acc[:, 0 : 2 * NC].rearrange("p (h c) -> p h c", h=2),
                    in1=bias_small,
                    op=ADD,
                )
                for dst, src in store_small.get(t, []):
                    nc.sync.dma_start(out=dst, in_=src)

        runs = []
        q0 = 0
        for n in RUNS:
            runs.append(list(range(q0, q0 + n)))
            q0 += n
        assert q0 * 2 == TILES

        for q in runs[0]:
            transposes(q)
        for q in runs[0]:
            exits(q)
        for q in runs[0]:
            quantise(q)
        for k, cur in enumerate(runs):
            nxt = runs[k + 1] if k + 1 < len(runs) else []
            for q in nxt:
                transposes(q)
            for q in nxt:
                exits(q)
            if k == 0:
                bias_spread()
            for q in cur:
                passes(q)
            for i in range(max(len(cur), len(nxt))):
                if i < len(nxt):
                    quantise(nxt[i])
                if i < len(cur):
                    finish(cur[i])
